import numpy as np
import ml_dtypes


def mxq(x, axis, fmt="e4m3"):
    dtype, down = {"e4m3": (ml_dtypes.float8_e4m3fn, 7), "e5m2": (ml_dtypes.float8_e5m2, 14)}[fmt]
    v = np.moveaxis(np.asarray(x, np.float32).astype(ml_dtypes.bfloat16).astype(np.float64), axis, -1)
    blocks = v.reshape(v.shape[:-1] + (-1, 32))
    amax = np.abs(blocks).max(-1, keepdims=True)
    byte = np.maximum(np.where(amax > 0, np.frexp(amax)[1] - 1 + 127, 0) - down, 1)
    scale = np.exp2(byte - 127.0)
    codes = (blocks / scale).astype(np.float32).astype(dtype).astype(np.float64)
    return np.moveaxis((codes * scale).reshape(v.shape), -1, axis)


WIDE = False


def mx_kscale(k):
    if not WIDE:
        return np.ones(k)
    levels = np.array([10, -10, 5, -5, 0])
    a = np.random.permutation(np.resize(levels, k // 512 * 4)).reshape(k // 512, 4)
    idx = np.arange(k)
    return np.exp2(a[idx // 512, idx % 128 // 32])


BF16 = ml_dtypes.bfloat16


def bf(x):
    return np.asarray(x, np.float32).astype(BF16)


def f64(x):
    return np.asarray(x).astype(np.float64)


B, D, N, L = 16384, 512, 128, 4
BN_EPS = 1e-5


def setup_inputs():
    t = mx_kscale(D)
    return {"h_lin": bf(np.random.standard_normal((B, D)) * 0.6 + np.random.standard_normal(D) * 0.5),
            "gamma": bf(np.random.uniform(0.5, 1.5, D) * t),
            "beta": bf(np.random.standard_normal(D) * 0.2 * t),
            "w": bf(np.random.standard_normal((D, N)) / np.sqrt(D) / t[:, None]),
            "b": bf(np.random.standard_normal(N) * 0.2)}


def reference(h_lin, gamma, beta, w, b):
    z = f64(h_lin)
    mu = z.mean(0)
    var = ((z - mu) ** 2).mean(0)
    h = np.maximum((z - mu) / np.sqrt(var + BN_EPS) * f64(gamma) + f64(beta), 0.0)
    return (mxq(h, 1, "e4m3") @ mxq(f64(w), 0, "e4m3")) + f64(b)

@@ -1,0 +1,253 @@
+from contextlib import ExitStack
+
+import concourse.masks as masks
+import concourse.mybir as mybir
+
+F32 = mybir.dt.float32
+BF16 = mybir.dt.bfloat16
+U32 = mybir.dt.uint32
+U8 = mybir.dt.uint8
+FP8X4 = mybir.dt.float8_e4m3fn_x4
+FUNC = mybir.ActivationFunctionType
+ALU = mybir.AluOpType
+AXIS = mybir.AxisListType
+
+P = 128
+PACK = 4
+ROWS = 16384
+K = 512
+N_OUT = 128
+BN_EPS = 1e-5
+
+BLOCKS = ROWS // P
+GROUP = 4
+GROUPS = BLOCKS // GROUP
+GROUP_ROWS = GROUP * P
+HALF_K = K // 2
+BN_STATS_MAX = 512
+BN_CALLS = 2 * GROUP_ROWS // BN_STATS_MAX
+AHEAD = 2
+
+FLOPS = 2 * ROWS * K * N_OUT
+
+
+def tile_customnetwork_pa_t_kernel(tc, h_lin, gamma, beta, w, b, out):
+    nc = tc.nc
+    x_dram = h_lin.rearrange("(p a) k -> p a k", a=BLOCKS)
+    out_dram = out.rearrange("(p a) n -> p a n", a=BLOCKS)
+
+    with ExitStack() as stack:
+        const = stack.enter_context(tc.tile_pool(name="const", bufs=1))
+        resident = stack.enter_context(tc.tile_pool(name="resident", bufs=GROUPS))
+        unread = stack.enter_context(tc.tile_pool(name="unread", bufs=4))
+        stage = stack.enter_context(tc.tile_pool(name="stage", bufs=3))
+        results = stack.enter_context(tc.tile_pool(name="results", bufs=4))
+        psum_x = stack.enter_context(tc.psum_pool(name="psum_x", bufs=6))
+        psum_acc = stack.enter_context(tc.psum_pool(name="psum_acc", bufs=2))
+        stack.enter_context(tc.manual_schedule())
+
+        eps = const.tile([P, 1], F32)
+        nc.vector.memset(eps[:], BN_EPS)
+        ones = const.tile([P, 2], BF16)
+        nc.vector.memset(ones[:], 1.0)
+        gb_rows = const.tile([P, HALF_K], BF16)
+        nc.vector.memset(gb_rows[:], 0.0)
+        ident = const.tile([P, P], F32)
+        masks.make_identity(nc, ident[:])
+
+        nc.scalar.dma_start(out=gb_rows[0:2, :], in_=gamma.rearrange("(u c) -> u c", u=2))
+        nc.scalar.dma_start(out=gb_rows[2:4, :], in_=beta.rearrange("(u c) -> u c", u=2))
+        w_planes = const.tile([P, PACK, N_OUT], BF16)
+        nc.scalar.dma_start(
+            out=w_planes[:].rearrange("p (u e) n -> p u (e n)", u=2),
+            in_=w.rearrange("(u p e) n -> p u (e n)", u=2, e=2),
+        )
+        warm = const.tile([P, 1], F32)
+        nc.scalar.activation(out=warm[:], in_=eps[:], func=FUNC.Sqrt)
+
+        x_tiles = []
+        for g in range(GROUPS):
+            x_g = resident.tile([P, GROUP, K], BF16, name="x_g")
+            nc.sync.dma_start(out=x_g[:], in_=x_dram[:, g * GROUP : (g + 1) * GROUP, :])
+            x_tiles.append(x_g)
+        b_rows = const.tile([P, N_OUT], BF16)
+        nc.sync.dma_start(out=b_rows[:], in_=b.partition_broadcast(P))
+
+        def transpose_half(g, u):
+            words = x_tiles[g][:].bitcast(F32)
+            xt = psum_x.tile([P, GROUP_ROWS], F32, name="xt")
+            for j in range(GROUP):
+                nc.tensor.transpose(
+                    xt[:, j * P : (j + 1) * P], words[:, j, u * P : (u + 1) * P], ident[:]
+                )
+            return xt
+
+        def one_k(xt, e):
+            return xt[:].bitcast(BF16).rearrange("p (r e) -> p r e", e=2)[:, :, e]
+
+        low_stats = const.tile([P, GROUPS * BN_CALLS, 6], F32)
+        shift_stats = const.tile([P, 2, 3], F32)
+        neg_shift = const.tile([P, 2], F32)
+        square_sums = const.tile([P, 2, GROUPS], F32)
+        plain_sums = psum_acc.tile([P, GROUPS, 2, 2], F32, name="acc")
+
+        for g in range(GROUPS):
+            xt_high = transpose_half(g, 1)
+            if g == 0:
+                nc.vector.bn_stats(
+                    out=shift_stats[:].rearrange("p e s -> p (e s)"),
+                    in_=xt_high[:].bitcast(BF16)[:, 0:BN_STATS_MAX],
+                )
+                nc.vector.tensor_scalar(
+                    out=neg_shift[:], in0=shift_stats[:, :, 1], scalar1=-1.0, scalar2=None, op0=ALU.mult
+                )
+            for e in range(2):
+                squares = unread.tile([P, GROUP_ROWS], BF16, name="squares")
+                nc.scalar.activation(
+                    out=squares[:],
+                    in_=one_k(xt_high, e),
+                    func=FUNC.Square,
+                    bias=neg_shift[:, e : e + 1],
+                    scale=1.0,
+                    accum_out=square_sums[:, e, g : g + 1],
+                )
+            for e in range(2):
+                for j in range(GROUP):
+                    nc.tensor.matmul(
+                        out=plain_sums[:, g, e, :],
+                        lhsT=x_tiles[g][:, j, HALF_K:K].rearrange("p (m e) -> p m e", e=2)[:, :, e],
+                        rhs=ones[:],
+                        start=(j == 0),
+                        stop=(j == GROUP - 1),
+                    )
+            xt_low = transpose_half(g, 0)
+            for i in range(BN_CALLS):
+                nc.vector.bn_stats(
+                    out=low_stats[:, g * BN_CALLS + i, :],
+                    in_=xt_low[:].bitcast(BF16)[:, i * BN_STATS_MAX : (i + 1) * BN_STATS_MAX],
+                )
+
+        gb_t = psum_x.tile([P, GROUP_ROWS], F32, name="xt")
+        nc.tensor.transpose(gb_t[:, 0:P], gb_rows[:].bitcast(F32), ident[:])
+        gamma_beta = const.tile([P, 2, PACK], F32)
+        nc.vector.tensor_copy(
+            out=gamma_beta[:].rearrange("p g t -> p (g t)"), in_=gb_t[:].bitcast(BF16)[:, 0 : 2 * PACK]
+        )
+
+        w_grouped = const.tile([P, N_OUT, PACK], BF16, align_bytes=64)
+        nc.vector.tensor_copy(out=w_grouped[:], in_=w_planes[:].rearrange("p t n -> p n t"))
+        w_codes = const.tile([P, N_OUT], U32, align_bytes=64)
+        w_scales = const.tile([P, N_OUT], U8, align_bytes=64)
+        nc.vector.quantize_mx(
+            out=w_codes[:].bitcast(FP8X4),
+            scales=w_scales[:],
+            in_=w_grouped[:].rearrange("p n t -> p (n t)"),
+        )
+
+        xt_of = {}
+        for g in range(AHEAD):
+            xt_of[g] = [transpose_half(g, 0), transpose_half(g, 1)]
+
+        mean_var = const.tile([P, PACK, 2], F32)
+        for e in range(2):
+            nc.vector.bn_aggr(out=mean_var[:, e, :], in_=low_stats[:, :, 3 * e : 3 * e + 3])
+        high_sum = const.tile([P, 2], F32)
+        nc.vector.tensor_reduce(
+            out=high_sum[:], in_=plain_sums[:, :, :, 0].rearrange("p g e -> p e g"), axis=AXIS.X, op=ALU.add
+        )
+        nc.vector.tensor_scalar(
+            out=mean_var[:, 2:4, 0], in0=high_sum[:], scalar1=1.0 / ROWS, scalar2=None, op0=ALU.mult
+        )
+        off_centre = const.tile([P, 2], F32)
+        nc.vector.tensor_tensor(out=off_centre[:], in0=mean_var[:, 2:4, 0], in1=neg_shift[:], op=ALU.add)
+        off_centre_sq = const.tile([P, 2], F32)
+        nc.vector.tensor_tensor(out=off_centre_sq[:], in0=off_centre[:], in1=off_centre[:], op=ALU.mult)
+        high_square_sum = const.tile([P, 2], F32)
+        nc.vector.tensor_reduce(out=high_square_sum[:], in_=square_sums[:], axis=AXIS.X, op=ALU.add)
+        nc.vector.scalar_tensor_tensor(
+            out=mean_var[:, 2:4, 1],
+            in0=high_square_sum[:],
+            scalar=1.0 / ROWS,
+            in1=off_centre_sq[:],
+            op0=ALU.mult,
+            op1=ALU.subtract,
+        )
+        std = const.tile([P, PACK], F32)
+        nc.scalar.activation(out=std[:], in_=mean_var[:, :, 1], func=FUNC.Sqrt, bias=eps[:], scale=1.0)
+        inv_std = const.tile([P, PACK], F32)
+        nc.vector.reciprocal(out=inv_std[:], in_=std[:])
+        scale_k = const.tile([P, PACK], F32)
+        nc.vector.tensor_tensor(out=scale_k[:], in0=gamma_beta[:, 0, :], in1=inv_std[:], op=ALU.mult)
+        mean_scaled = const.tile([P, PACK], F32)
+        nc.vector.tensor_tensor(out=mean_scaled[:], in0=mean_var[:, :, 0], in1=scale_k[:], op=ALU.mult)
+        offset_k = const.tile([P, PACK], F32)
+        nc.vector.tensor_tensor(out=offset_k[:], in0=gamma_beta[:, 1, :], in1=mean_scaled[:], op=ALU.subtract)
+
+        planes_of = {}
+        grouped_of = {}
+        acc_of = {}
+
+        def normalise(g):
+            planes = stage.tile([P, PACK, GROUP_ROWS], BF16, name="planes")
+            for u in range(2):
+                for e in range(2):
+                    t = 2 * u + e
+                    nc.scalar.activation(
+                        out=planes[:, t, :],
+                        in_=one_k(xt_of[g][u], e),
+                        func=FUNC.Relu,
+                        bias=offset_k[:, t : t + 1],
+                        scale=scale_k[:, t : t + 1],
+                    )
+            planes_of[g] = planes
+
+        def interleave(g):
+            grouped = stage.tile([P, GROUP_ROWS, PACK], BF16, name="grouped", align_bytes=64)
+            nc.vector.tensor_copy(
+                out=grouped[:].rearrange("p (c i) t -> p c t i", i=4),
+                in_=planes_of[g][:].rearrange("p t (c i) -> p c t i", i=4),
+            )
+            grouped_of[g] = grouped
+
+        def quantise_and_multiply(g):
+            codes = stage.tile([P, GROUP_ROWS], U32, name="codes", align_bytes=64)
+            scales = stage.tile([P, GROUP_ROWS], U8, name="scales", align_bytes=64)
+            nc.vector.quantize_mx(
+                out=codes[:].bitcast(FP8X4),
+                scales=scales[:],
+                in_=grouped_of[g][:].rearrange("p r t -> p (r t)"),
+            )
+            acc = psum_acc.tile([P, GROUP, N_OUT], F32, name="acc")
+            for j in range(GROUP):
+                block = slice(j * P, (j + 1) * P)
+                nc.tensor.matmul_mx(
+                    out=acc[:, j, :],
+                    lhsT=codes[:, block].bitcast(FP8X4),
+                    lhsT_scale=scales[:, block],
+                    rhs=w_codes[:].bitcast(FP8X4),
+                    rhs_scale=w_scales[:],
+                    start=True,
+                    stop=True,
+                )
+            acc_of[g] = acc
+
+        def add_bias_and_store(g):
+            result = results.tile([P, GROUP, N_OUT], F32, name="result")
+            nc.vector.tensor_tensor(
+                out=result[:],
+                in0=acc_of[g][:],
+                in1=b_rows[:].unsqueeze(1).to_broadcast([P, GROUP, N_OUT]),
+                op=ALU.add,
+            )
+            nc.sync.dma_start(out=out_dram[:, g * GROUP : (g + 1) * GROUP, :], in_=result[:])
+
+        for s in range(GROUPS + 2):
+            if s + AHEAD < GROUPS:
+                xt_of[s + AHEAD] = [transpose_half(s + AHEAD, 0), transpose_half(s + AHEAD, 1)]
+            if s < GROUPS:
+                normalise(s)
+                interleave(s)
+            if 1 <= s <= GROUPS:
+                quantise_and_multiply(s - 1)
+            if s >= 2:
+                add_bias_and_store(s - 2)

@@ -26,6 +26,7 @@ GROUP_ROWS = GROUP * P
 HALF_K = K // 2
 BN_STATS_MAX = 512
 BN_CALLS = 2 * GROUP_ROWS // BN_STATS_MAX
+SCALAR_OF_8 = 5
 AHEAD = 2
 
 FLOPS = 2 * ROWS * K * N_OUT
@@ -48,8 +49,6 @@ def tile_customnetwork_pa_t_kernel(tc, h_lin, gamma, beta, w, b, out):
 
         eps = const.tile([P, 1], F32)
         nc.vector.memset(eps[:], BN_EPS)
-        ones = const.tile([P, 2], BF16)
-        nc.vector.memset(ones[:], 1.0)
         gb_rows = const.tile([P, HALF_K], BF16)
         nc.vector.memset(gb_rows[:], 0.0)
         ident = const.tile([P, P], F32)
@@ -85,12 +84,24 @@ def tile_customnetwork_pa_t_kernel(tc, h_lin, gamma, beta, w, b, out):
         def one_k(xt, e):
             return xt[:].bitcast(BF16).rearrange("p (r e) -> p r e", e=2)[:, :, e]
 
-        low_stats = const.tile([P, GROUPS * BN_CALLS, 6], F32)
+        scalar_groups = [g for g in range(GROUPS) if (SCALAR_OF_8 * g) % 8 < SCALAR_OF_8]
+        scalar_rows = len(scalar_groups) * GROUP_ROWS
+        high_calls = (GROUPS - len(scalar_groups)) * BN_CALLS
+        low_stats = const.tile([P, GROUPS * BN_CALLS, 2, 3], F32)
+        high_stats = const.tile([P, high_calls + 1, 2, 3], F32)
+        nc.vector.memset(high_stats[:, high_calls, :, :], float(scalar_rows))
         shift_stats = const.tile([P, 2, 3], F32)
         neg_shift = const.tile([P, 2], F32)
-        square_sums = const.tile([P, 2, GROUPS], F32)
-        plain_sums = psum_acc.tile([P, GROUPS, 2, 2], F32, name="acc")
+        scalar_sums = const.tile([P, 2, 2, len(scalar_groups)], F32)
 
+        def vector_stats(xt, stats, first):
+            for i in range(BN_CALLS):
+                nc.vector.bn_stats(
+                    out=stats[:, first + i, :, :].rearrange("p e s -> p (e s)"),
+                    in_=xt[:].bitcast(BF16)[:, i * BN_STATS_MAX : (i + 1) * BN_STATS_MAX],
+                )
+
+        high_done = 0
         for g in range(GROUPS):
             xt_high = transpose_half(g, 1)
             if g == 0:
@@ -101,31 +112,24 @@ def tile_customnetwork_pa_t_kernel(tc, h_lin, gamma, beta, w, b, out):
                 nc.vector.tensor_scalar(
                     out=neg_shift[:], in0=shift_stats[:, :, 1], scalar1=-1.0, scalar2=None, op0=ALU.mult
                 )
-            for e in range(2):
-                squares = unread.tile([P, GROUP_ROWS], BF16, name="squares")
-                nc.scalar.activation(
-                    out=squares[:],
-                    in_=one_k(xt_high, e),
-                    func=FUNC.Square,
-                    bias=neg_shift[:, e : e + 1],
-                    scale=1.0,
-                    accum_out=square_sums[:, e, g : g + 1],
-                )
-            for e in range(2):
-                for j in range(GROUP):
-                    nc.tensor.matmul(
-                        out=plain_sums[:, g, e, :],
-                        lhsT=x_tiles[g][:, j, HALF_K:K].rearrange("p (m e) -> p m e", e=2)[:, :, e],
-                        rhs=ones[:],
-                        start=(j == 0),
-                        stop=(j == GROUP - 1),
-                    )
+            if g in scalar_groups:
+                for power, func in enumerate((FUNC.Identity, FUNC.Square)):
+                    for e in range(2):
+                        unread_out = unread.tile([P, GROUP_ROWS], BF16, name="unread_out")
+                        i = scalar_groups.index(g)
+                        nc.scalar.activation(
+                            out=unread_out[:],
+                            in_=one_k(xt_high, e),
+                            func=func,
+                            bias=neg_shift[:, e : e + 1],
+                            scale=1.0,
+                            accum_out=scalar_sums[:, power, e, i : i + 1],
+                        )
+            else:
+                vector_stats(xt_high, high_stats, high_done)
+                high_done += BN_CALLS
             xt_low = transpose_half(g, 0)
-            for i in range(BN_CALLS):
-                nc.vector.bn_stats(
-                    out=low_stats[:, g * BN_CALLS + i, :],
-                    in_=xt_low[:].bitcast(BF16)[:, i * BN_STATS_MAX : (i + 1) * BN_STATS_MAX],
-                )
+            vector_stats(xt_low, low_stats, g * BN_CALLS)
 
         gb_t = psum_x.tile([P, GROUP_ROWS], F32, name="xt")
         nc.tensor.transpose(gb_t[:, 0:P], gb_rows[:].bitcast(F32), ident[:])
@@ -150,28 +154,23 @@ def tile_customnetwork_pa_t_kernel(tc, h_lin, gamma, beta, w, b, out):
 
         mean_var = const.tile([P, PACK, 2], F32)
         for e in range(2):
-            nc.vector.bn_aggr(out=mean_var[:, e, :], in_=low_stats[:, :, 3 * e : 3 * e + 3])
-        high_sum = const.tile([P, 2], F32)
-        nc.vector.tensor_reduce(
-            out=high_sum[:], in_=plain_sums[:, :, :, 0].rearrange("p g e -> p e g"), axis=AXIS.X, op=ALU.add
-        )
-        nc.vector.tensor_scalar(
-            out=mean_var[:, 2:4, 0], in0=high_sum[:], scalar1=1.0 / ROWS, scalar2=None, op0=ALU.mult
-        )
+            nc.vector.bn_aggr(out=mean_var[:, e, :], in_=low_stats[:, :, e, :])
+        totals = const.tile([P, 2, 2], F32)
+        nc.vector.tensor_reduce(out=totals[:], in_=scalar_sums[:], axis=AXIS.X, op=ALU.add)
         off_centre = const.tile([P, 2], F32)
-        nc.vector.tensor_tensor(out=off_centre[:], in0=mean_var[:, 2:4, 0], in1=neg_shift[:], op=ALU.add)
-        off_centre_sq = const.tile([P, 2], F32)
-        nc.vector.tensor_tensor(out=off_centre_sq[:], in0=off_centre[:], in1=off_centre[:], op=ALU.mult)
-        high_square_sum = const.tile([P, 2], F32)
-        nc.vector.tensor_reduce(out=high_square_sum[:], in_=square_sums[:], axis=AXIS.X, op=ALU.add)
-        nc.vector.scalar_tensor_tensor(
-            out=mean_var[:, 2:4, 1],
-            in0=high_square_sum[:],
-            scalar=1.0 / ROWS,
-            in1=off_centre_sq[:],
-            op0=ALU.mult,
-            op1=ALU.subtract,
+        nc.vector.tensor_scalar(
+            out=off_centre[:], in0=totals[:, 0, :], scalar1=1.0 / scalar_rows, scalar2=None, op0=ALU.mult
         )
+        nc.vector.tensor_tensor(
+            out=high_stats[:, high_calls, :, 1], in0=off_centre[:], in1=neg_shift[:], op=ALU.subtract
+        )
+        correction = const.tile([P, 2], F32)
+        nc.vector.tensor_tensor(out=correction[:], in0=totals[:, 0, :], in1=off_centre[:], op=ALU.mult)
+        nc.vector.tensor_tensor(
+            out=high_stats[:, high_calls, :, 2], in0=totals[:, 1, :], in1=correction[:], op=ALU.subtract
+        )
+        for e in range(2):
+            nc.vector.bn_aggr(out=mean_var[:, 2 + e, :], in_=high_stats[:, :, e, :])
         std = const.tile([P, PACK], F32)
         nc.scalar.activation(out=std[:], in_=mean_var[:, :, 1], func=FUNC.Sqrt, bias=eps[:], scale=1.0)
         inv_std = const.tile([P, PACK], F32)

@@ -26,7 +26,9 @@ GROUP_ROWS = GROUP * P
 HALF_K = K // 2
 BN_STATS_MAX = 512
 BN_CALLS = 2 * GROUP_ROWS // BN_STATS_MAX
-SCALAR_OF_8 = 5
+ONES = 2
+GPSIMD_BLOCKS = 2
+EARLY_GROUPS = 24
 AHEAD = 2
 
 FLOPS = 2 * ROWS * K * N_OUT
@@ -49,6 +51,12 @@ def tile_customnetwork_pa_t_kernel(tc, h_lin, gamma, beta, w, b, out):
 
         eps = const.tile([P, 1], F32)
         nc.vector.memset(eps[:], BN_EPS)
+        ones = const.tile([P, ONES], BF16)
+        nc.vector.memset(ones[:], 1.0)
+        ones_f32 = const.tile([P, ONES], F32)
+        nc.vector.memset(ones_f32[:], 1.0)
+        partition_sums = const.tile([P, GPSIMD_BLOCKS, HALF_K], F32)
+        nc.gpsimd.memset(partition_sums[:], 0.0)
         gb_rows = const.tile([P, HALF_K], BF16)
         nc.vector.memset(gb_rows[:], 0.0)
         ident = const.tile([P, P], F32)
@@ -84,24 +92,19 @@ def tile_customnetwork_pa_t_kernel(tc, h_lin, gamma, beta, w, b, out):
         def one_k(xt, e):
             return xt[:].bitcast(BF16).rearrange("p (r e) -> p r e", e=2)[:, :, e]
 
-        scalar_groups = [g for g in range(GROUPS) if (SCALAR_OF_8 * g) % 8 < SCALAR_OF_8]
-        scalar_rows = len(scalar_groups) * GROUP_ROWS
-        high_calls = (GROUPS - len(scalar_groups)) * BN_CALLS
-        low_stats = const.tile([P, GROUPS * BN_CALLS, 2, 3], F32)
-        high_stats = const.tile([P, high_calls + 1, 2, 3], F32)
-        nc.vector.memset(high_stats[:, high_calls, :, :], float(scalar_rows))
+        low_calls = GROUPS * BN_CALLS
+        early_calls = EARLY_GROUPS * BN_CALLS
+        early_rows = EARLY_GROUPS * GROUP_ROWS
+        low_stats = const.tile([P, low_calls + 1, 2, 3], F32)
+        nc.vector.memset(low_stats[:, low_calls, :, :], float(early_rows))
         shift_stats = const.tile([P, 2, 3], F32)
         neg_shift = const.tile([P, 2], F32)
-        scalar_sums = const.tile([P, 2, 2, len(scalar_groups)], F32)
+        square_sums = const.tile([P, 2, GROUPS], F32)
+        plain_sums = []
+        for e in range(2):
+            plain_sum = psum_acc.tile([P, ONES], F32, name="acc")
+            plain_sums.append(plain_sum)
 
-        def vector_stats(xt, stats, first):
-            for i in range(BN_CALLS):
-                nc.vector.bn_stats(
-                    out=stats[:, first + i, :, :].rearrange("p e s -> p (e s)"),
-                    in_=xt[:].bitcast(BF16)[:, i * BN_STATS_MAX : (i + 1) * BN_STATS_MAX],
-                )
-
-        high_done = 0
         for g in range(GROUPS):
             xt_high = transpose_half(g, 1)
             if g == 0:
@@ -112,24 +115,49 @@ def tile_customnetwork_pa_t_kernel(tc, h_lin, gamma, beta, w, b, out):
                 nc.vector.tensor_scalar(
                     out=neg_shift[:], in0=shift_stats[:, :, 1], scalar1=-1.0, scalar2=None, op0=ALU.mult
                 )
-            if g in scalar_groups:
-                for power, func in enumerate((FUNC.Identity, FUNC.Square)):
-                    for e in range(2):
-                        unread_out = unread.tile([P, GROUP_ROWS], BF16, name="unread_out")
-                        i = scalar_groups.index(g)
-                        nc.scalar.activation(
-                            out=unread_out[:],
-                            in_=one_k(xt_high, e),
-                            func=func,
-                            bias=neg_shift[:, e : e + 1],
-                            scale=1.0,
-                            accum_out=scalar_sums[:, power, e, i : i + 1],
-                        )
-            else:
-                vector_stats(xt_high, high_stats, high_done)
-                high_done += BN_CALLS
+            for e in range(2):
+                squares = unread.tile([P, GROUP_ROWS], BF16, name="squares")
+                nc.scalar.activation(
+                    out=squares[:],
+                    in_=one_k(xt_high, e),
+                    func=FUNC.Square,
+                    bias=neg_shift[:, e : e + 1],
+                    scale=1.0,
+                    accum_out=square_sums[:, e, g : g + 1],
+                )
+            nc.gpsimd.tensor_tensor(
+                out=partition_sums[:],
+                in0=partition_sums[:],
+                in1=x_tiles[g][:, 0:GPSIMD_BLOCKS, HALF_K:K],
+                op=ALU.add,
+            )
+            for e in range(2):
+                for j in range(GPSIMD_BLOCKS, GROUP):
+                    nc.tensor.matmul(
+                        out=plain_sums[e][:],
+                        lhsT=x_tiles[g][:, j, HALF_K:K].rearrange("p (m e) -> p m e", e=2)[:, :, e],
+                        rhs=ones[:],
+                        start=(g == 0 and j == GPSIMD_BLOCKS),
+                        stop=False,
+                    )
             xt_low = transpose_half(g, 0)
-            vector_stats(xt_low, low_stats, g * BN_CALLS)
+            for i in range(BN_CALLS):
+                nc.vector.bn_stats(
+                    out=low_stats[:, g * BN_CALLS + i, :, :].rearrange("p e s -> p (e s)"),
+                    in_=xt_low[:].bitcast(BF16)[:, i * BN_STATS_MAX : (i + 1) * BN_STATS_MAX],
+                )
+            if g == EARLY_GROUPS - 1:
+                for e in range(2):
+                    nc.vector.bn_aggr(
+                        out=low_stats[:, low_calls, e, 1:3], in_=low_stats[:, 0:early_calls, e, :]
+                    )
+                nc.vector.tensor_scalar(
+                    out=low_stats[:, low_calls, :, 2],
+                    in0=low_stats[:, low_calls, :, 2],
+                    scalar1=float(early_rows),
+                    scalar2=None,
+                    op0=ALU.mult,
+                )
 
         gb_t = psum_x.tile([P, GROUP_ROWS], F32, name="xt")
         nc.tensor.transpose(gb_t[:, 0:P], gb_rows[:].bitcast(F32), ident[:])
@@ -138,15 +166,15 @@ def tile_customnetwork_pa_t_kernel(tc, h_lin, gamma, beta, w, b, out):
             out=gamma_beta[:].rearrange("p g t -> p (g t)"), in_=gb_t[:].bitcast(BF16)[:, 0 : 2 * PACK]
         )
 
-        w_grouped = const.tile([P, N_OUT, PACK], BF16, align_bytes=64)
-        nc.vector.tensor_copy(out=w_grouped[:], in_=w_planes[:].rearrange("p t n -> p n t"))
-        w_codes = const.tile([P, N_OUT], U32, align_bytes=64)
-        w_scales = const.tile([P, N_OUT], U8, align_bytes=64)
-        nc.vector.quantize_mx(
-            out=w_codes[:].bitcast(FP8X4),
-            scales=w_scales[:],
-            in_=w_grouped[:].rearrange("p n t -> p (n t)"),
-        )
+        for e in range(2):
+            for j in range(GPSIMD_BLOCKS):
+                nc.tensor.matmul(
+                    out=plain_sums[e][:],
+                    lhsT=partition_sums[:, j, :].rearrange("p (m e) -> p m e", e=2)[:, :, e],
+                    rhs=ones_f32[:],
+                    start=False,
+                    stop=(j == GPSIMD_BLOCKS - 1),
+                )
 
         xt_of = {}
         for g in range(AHEAD):
@@ -154,23 +182,25 @@ def tile_customnetwork_pa_t_kernel(tc, h_lin, gamma, beta, w, b, out):
 
         mean_var = const.tile([P, PACK, 2], F32)
         for e in range(2):
-            nc.vector.bn_aggr(out=mean_var[:, e, :], in_=low_stats[:, :, e, :])
-        totals = const.tile([P, 2, 2], F32)
-        nc.vector.tensor_reduce(out=totals[:], in_=scalar_sums[:], axis=AXIS.X, op=ALU.add)
-        off_centre = const.tile([P, 2], F32)
-        nc.vector.tensor_scalar(
-            out=off_centre[:], in0=totals[:, 0, :], scalar1=1.0 / scalar_rows, scalar2=None, op0=ALU.mult
-        )
-        nc.vector.tensor_tensor(
-            out=high_stats[:, high_calls, :, 1], in0=off_centre[:], in1=neg_shift[:], op=ALU.subtract
-        )
-        correction = const.tile([P, 2], F32)
-        nc.vector.tensor_tensor(out=correction[:], in0=totals[:, 0, :], in1=off_centre[:], op=ALU.mult)
-        nc.vector.tensor_tensor(
-            out=high_stats[:, high_calls, :, 2], in0=totals[:, 1, :], in1=correction[:], op=ALU.subtract
-        )
+            nc.vector.bn_aggr(out=mean_var[:, e, :], in_=low_stats[:, early_calls : low_calls + 1, e, :])
         for e in range(2):
-            nc.vector.bn_aggr(out=mean_var[:, 2 + e, :], in_=high_stats[:, :, e, :])
+            nc.vector.tensor_scalar(
+                out=mean_var[:, 2 + e, 0:1], in0=plain_sums[e][:, 0:1], scalar1=1.0 / ROWS, scalar2=None, op0=ALU.mult
+            )
+        off_centre = const.tile([P, 2], F32)
+        nc.vector.tensor_tensor(out=off_centre[:], in0=mean_var[:, 2:4, 0], in1=neg_shift[:], op=ALU.add)
+        off_centre_sq = const.tile([P, 2], F32)
+        nc.vector.tensor_tensor(out=off_centre_sq[:], in0=off_centre[:], in1=off_centre[:], op=ALU.mult)
+        high_square_sum = const.tile([P, 2], F32)
+        nc.vector.tensor_reduce(out=high_square_sum[:], in_=square_sums[:], axis=AXIS.X, op=ALU.add)
+        nc.vector.scalar_tensor_tensor(
+            out=mean_var[:, 2:4, 1],
+            in0=high_square_sum[:],
+            scalar=1.0 / ROWS,
+            in1=off_centre_sq[:],
+            op0=ALU.mult,
+            op1=ALU.subtract,
+        )
         std = const.tile([P, PACK], F32)
         nc.scalar.activation(out=std[:], in_=mean_var[:, :, 1], func=FUNC.Sqrt, bias=eps[:], scale=1.0)
         inv_std = const.tile([P, PACK], F32)
@@ -181,6 +211,16 @@ def tile_customnetwork_pa_t_kernel(tc, h_lin, gamma, beta, w, b, out):
         nc.vector.tensor_tensor(out=mean_scaled[:], in0=mean_var[:, :, 0], in1=scale_k[:], op=ALU.mult)
         offset_k = const.tile([P, PACK], F32)
         nc.vector.tensor_tensor(out=offset_k[:], in0=gamma_beta[:, 1, :], in1=mean_scaled[:], op=ALU.subtract)
+
+        w_grouped = const.tile([P, N_OUT, PACK], BF16, align_bytes=64)
+        nc.vector.tensor_copy(out=w_grouped[:], in_=w_planes[:].rearrange("p t n -> p n t"))
+        w_codes = const.tile([P, N_OUT], U32, align_bytes=64)
+        w_scales = const.tile([P, N_OUT], U8, align_bytes=64)
+        nc.vector.quantize_mx(
+            out=w_codes[:].bitcast(FP8X4),
+            scales=w_scales[:],
+            in_=w_grouped[:].rearrange("p n t -> p (n t)"),
+        )
 
         planes_of = {}
         grouped_of = {}

@@ -75,7 +75,11 @@ def tile_customnetwork_pa_t_kernel(tc, h_lin, gamma, beta, w, b, out):
         x_tiles = []
         for g in range(GROUPS):
             x_g = resident.tile([P, GROUP, K], BF16, name="x_g")
-            nc.sync.dma_start(out=x_g[:], in_=x_dram[:, g * GROUP : (g + 1) * GROUP, :])
+            if g == 0:
+                for j in range(GROUP):
+                    nc.sync.dma_start(out=x_g[:, j, :], in_=x_dram[:, j, :])
+            else:
+                nc.sync.dma_start(out=x_g[:], in_=x_dram[:, g * GROUP : (g + 1) * GROUP, :])
             x_tiles.append(x_g)
         b_rows = const.tile([P, N_OUT], BF16)
         nc.sync.dma_start(out=b_rows[:], in_=b.partition_broadcast(P))
@@ -106,6 +110,24 @@ def tile_customnetwork_pa_t_kernel(tc, h_lin, gamma, beta, w, b, out):
             plain_sums.append(plain_sum)
 
         for g in range(GROUPS):
+            xt_low = transpose_half(g, 0)
+            for i in range(BN_CALLS):
+                nc.vector.bn_stats(
+                    out=low_stats[:, g * BN_CALLS + i, :, :].rearrange("p e s -> p (e s)"),
+                    in_=xt_low[:].bitcast(BF16)[:, i * BN_STATS_MAX : (i + 1) * BN_STATS_MAX],
+                )
+            if g == EARLY_GROUPS - 1:
+                for e in range(2):
+                    nc.vector.bn_aggr(
+                        out=low_stats[:, low_calls, e, 1:3], in_=low_stats[:, 0:early_calls, e, :]
+                    )
+                nc.vector.tensor_scalar(
+                    out=low_stats[:, low_calls, :, 2],
+                    in0=low_stats[:, low_calls, :, 2],
+                    scalar1=float(early_rows),
+                    scalar2=None,
+                    op0=ALU.mult,
+                )
             xt_high = transpose_half(g, 1)
             if g == 0:
                 nc.vector.bn_stats(
@@ -140,24 +162,6 @@ def tile_customnetwork_pa_t_kernel(tc, h_lin, gamma, beta, w, b, out):
                         start=(g == 0 and j == GPSIMD_BLOCKS),
                         stop=False,
                     )
-            xt_low = transpose_half(g, 0)
-            for i in range(BN_CALLS):
-                nc.vector.bn_stats(
-                    out=low_stats[:, g * BN_CALLS + i, :, :].rearrange("p e s -> p (e s)"),
-                    in_=xt_low[:].bitcast(BF16)[:, i * BN_STATS_MAX : (i + 1) * BN_STATS_MAX],
-                )
-            if g == EARLY_GROUPS - 1:
-                for e in range(2):
-                    nc.vector.bn_aggr(
-                        out=low_stats[:, low_calls, e, 1:3], in_=low_stats[:, 0:early_calls, e, :]
-                    )
-                nc.vector.tensor_scalar(
-                    out=low_stats[:, low_calls, :, 2],
-                    in0=low_stats[:, low_calls, :, 2],
-                    scalar1=float(early_rows),
-                    scalar2=None,
-                    op0=ALU.mult,
-                )
 
         gb_t = psum_x.tile([P, GROUP_ROWS], F32, name="xt")
         nc.tensor.transpose(gb_t[:, 0:P], gb_rows[:].bitcast(F32), ident[:])
@@ -280,13 +284,13 @@ def tile_customnetwork_pa_t_kernel(tc, h_lin, gamma, beta, w, b, out):
             )
             nc.sync.dma_start(out=out_dram[:, g * GROUP : (g + 1) * GROUP, :], in_=result[:])
 
-        for s in range(GROUPS + 2):
+        for s in range(GROUPS + 1):
             if s + AHEAD < GROUPS:
                 xt_of[s + AHEAD] = [transpose_half(s + AHEAD, 0), transpose_half(s + AHEAD, 1)]
             if s < GROUPS:
                 normalise(s)
                 interleave(s)
-            if 1 <= s <= GROUPS:
-                quantise_and_multiply(s - 1)
-            if s >= 2:
-                add_bias_and_store(s - 2)
+            if s >= 1:
+                add_bias_and_store(s - 1)
+            if s < GROUPS:
+                quantise_and_multiply(s)

@@ -284,13 +284,13 @@ def tile_customnetwork_pa_t_kernel(tc, h_lin, gamma, beta, w, b, out):
             )
             nc.sync.dma_start(out=out_dram[:, g * GROUP : (g + 1) * GROUP, :], in_=result[:])
 
-        for s in range(GROUPS + 1):
+        for s in range(GROUPS + 2):
             if s + AHEAD < GROUPS:
                 xt_of[s + AHEAD] = [transpose_half(s + AHEAD, 0), transpose_half(s + AHEAD, 1)]
             if s < GROUPS:
                 normalise(s)
                 interleave(s)
-            if s >= 1:
-                add_bias_and_store(s - 1)
-            if s < GROUPS:
-                quantise_and_multiply(s)
+            if 1 <= s <= GROUPS:
+                quantise_and_multiply(s - 1)
+            if s >= 2:
+                add_bias_and_store(s - 2)

from contextlib import ExitStack

import concourse.masks as masks
import concourse.mybir as mybir

F32 = mybir.dt.float32
BF16 = mybir.dt.bfloat16
U32 = mybir.dt.uint32
U8 = mybir.dt.uint8
FP8X4 = mybir.dt.float8_e4m3fn_x4
FUNC = mybir.ActivationFunctionType
ALU = mybir.AluOpType
AXIS = mybir.AxisListType

P = 128
PACK = 4
ROWS = 16384
K = 512
N_OUT = 128
BN_EPS = 1e-5

BLOCKS = ROWS // P
GROUP = 4
GROUPS = BLOCKS // GROUP
GROUP_ROWS = GROUP * P
HALF_K = K // 2
BN_STATS_MAX = 512
BN_CALLS = 2 * GROUP_ROWS // BN_STATS_MAX
ONES = 2
GPSIMD_BLOCKS = 2
EARLY_GROUPS = 24
AHEAD = 2

FLOPS = 2 * ROWS * K * N_OUT


def tile_customnetwork_pa_t_kernel(tc, h_lin, gamma, beta, w, b, out):
    nc = tc.nc
    x_dram = h_lin.rearrange("(p a) k -> p a k", a=BLOCKS)
    out_dram = out.rearrange("(p a) n -> p a n", a=BLOCKS)

    with ExitStack() as stack:
        const = stack.enter_context(tc.tile_pool(name="const", bufs=1))
        resident = stack.enter_context(tc.tile_pool(name="resident", bufs=GROUPS))
        unread = stack.enter_context(tc.tile_pool(name="unread", bufs=4))
        stage = stack.enter_context(tc.tile_pool(name="stage", bufs=3))
        results = stack.enter_context(tc.tile_pool(name="results", bufs=4))
        psum_x = stack.enter_context(tc.psum_pool(name="psum_x", bufs=6))
        psum_acc = stack.enter_context(tc.psum_pool(name="psum_acc", bufs=2))
        stack.enter_context(tc.manual_schedule())

        eps = const.tile([P, 1], F32)
        nc.vector.memset(eps[:], BN_EPS)
        ones = const.tile([P, ONES], BF16)
        nc.vector.memset(ones[:], 1.0)
        ones_f32 = const.tile([P, ONES], F32)
        nc.vector.memset(ones_f32[:], 1.0)
        partition_sums = const.tile([P, GPSIMD_BLOCKS, HALF_K], F32)
        nc.gpsimd.memset(partition_sums[:], 0.0)
        gb_rows = const.tile([P, HALF_K], BF16)
        nc.vector.memset(gb_rows[:], 0.0)
        ident = const.tile([P, P], F32)
        masks.make_identity(nc, ident[:])

        nc.scalar.dma_start(out=gb_rows[0:2, :], in_=gamma.rearrange("(u c) -> u c", u=2))
        nc.scalar.dma_start(out=gb_rows[2:4, :], in_=beta.rearrange("(u c) -> u c", u=2))
        w_planes = const.tile([P, PACK, N_OUT], BF16)
        nc.scalar.dma_start(
            out=w_planes[:].rearrange("p (u e) n -> p u (e n)", u=2),
            in_=w.rearrange("(u p e) n -> p u (e n)", u=2, e=2),
        )
        warm = const.tile([P, 1], F32)
        nc.scalar.activation(out=warm[:], in_=eps[:], func=FUNC.Sqrt)

        x_tiles = []
        for g in range(GROUPS):
            x_g = resident.tile([P, GROUP, K], BF16, name="x_g")
            if g == 0:
                for j in range(GROUP):
                    nc.sync.dma_start(out=x_g[:, j, :], in_=x_dram[:, j, :])
            else:
                nc.sync.dma_start(out=x_g[:], in_=x_dram[:, g * GROUP : (g + 1) * GROUP, :])
            x_tiles.append(x_g)
        b_rows = const.tile([P, N_OUT], BF16)
        nc.sync.dma_start(out=b_rows[:], in_=b.partition_broadcast(P))

        def transpose_half(g, u):
            words = x_tiles[g][:].bitcast(F32)
            xt = psum_x.tile([P, GROUP_ROWS], F32, name="xt")
            for j in range(GROUP):
                nc.tensor.transpose(
                    xt[:, j * P : (j + 1) * P], words[:, j, u * P : (u + 1) * P], ident[:]
                )
            return xt

        def one_k(xt, e):
            return xt[:].bitcast(BF16).rearrange("p (r e) -> p r e", e=2)[:, :, e]

        low_calls = GROUPS * BN_CALLS
        early_calls = EARLY_GROUPS * BN_CALLS
        early_rows = EARLY_GROUPS * GROUP_ROWS
        low_stats = const.tile([P, low_calls + 1, 2, 3], F32)
        nc.vector.memset(low_stats[:, low_calls, :, :], float(early_rows))
        shift_stats = const.tile([P, 2, 3], F32)
        neg_shift = const.tile([P, 2], F32)
        square_sums = const.tile([P, 2, GROUPS], F32)
        plain_sums = []
        for e in range(2):
            plain_sum = psum_acc.tile([P, ONES], F32, name="acc")
            plain_sums.append(plain_sum)

        for g in range(GROUPS):
            xt_low = transpose_half(g, 0)
            for i in range(BN_CALLS):
                nc.vector.bn_stats(
                    out=low_stats[:, g * BN_CALLS + i, :, :].rearrange("p e s -> p (e s)"),
                    in_=xt_low[:].bitcast(BF16)[:, i * BN_STATS_MAX : (i + 1) * BN_STATS_MAX],
                )
            if g == EARLY_GROUPS - 1:
                for e in range(2):
                    nc.vector.bn_aggr(
                        out=low_stats[:, low_calls, e, 1:3], in_=low_stats[:, 0:early_calls, e, :]
                    )
                nc.vector.tensor_scalar(
                    out=low_stats[:, low_calls, :, 2],
                    in0=low_stats[:, low_calls, :, 2],
                    scalar1=float(early_rows),
                    scalar2=None,
                    op0=ALU.mult,
                )
            xt_high = transpose_half(g, 1)
            if g == 0:
                nc.vector.bn_stats(
                    out=shift_stats[:].rearrange("p e s -> p (e s)"),
                    in_=xt_high[:].bitcast(BF16)[:, 0:BN_STATS_MAX],
                )
                nc.vector.tensor_scalar(
                    out=neg_shift[:], in0=shift_stats[:, :, 1], scalar1=-1.0, scalar2=None, op0=ALU.mult
                )
            for e in range(2):
                squares = unread.tile([P, GROUP_ROWS], BF16, name="squares")
                nc.scalar.activation(
                    out=squares[:],
                    in_=one_k(xt_high, e),
                    func=FUNC.Square,
                    bias=neg_shift[:, e : e + 1],
                    scale=1.0,
                    accum_out=square_sums[:, e, g : g + 1],
                )
            nc.gpsimd.tensor_tensor(
                out=partition_sums[:],
                in0=partition_sums[:],
                in1=x_tiles[g][:, 0:GPSIMD_BLOCKS, HALF_K:K],
                op=ALU.add,
            )
            for e in range(2):
                for j in range(GPSIMD_BLOCKS, GROUP):
                    nc.tensor.matmul(
                        out=plain_sums[e][:],
                        lhsT=x_tiles[g][:, j, HALF_K:K].rearrange("p (m e) -> p m e", e=2)[:, :, e],
                        rhs=ones[:],
                        start=(g == 0 and j == GPSIMD_BLOCKS),
                        stop=False,
                    )

        gb_t = psum_x.tile([P, GROUP_ROWS], F32, name="xt")
        nc.tensor.transpose(gb_t[:, 0:P], gb_rows[:].bitcast(F32), ident[:])
        gamma_beta = const.tile([P, 2, PACK], F32)
        nc.vector.tensor_copy(
            out=gamma_beta[:].rearrange("p g t -> p (g t)"), in_=gb_t[:].bitcast(BF16)[:, 0 : 2 * PACK]
        )

        for e in range(2):
            for j in range(GPSIMD_BLOCKS):
                nc.tensor.matmul(
                    out=plain_sums[e][:],
                    lhsT=partition_sums[:, j, :].rearrange("p (m e) -> p m e", e=2)[:, :, e],
                    rhs=ones_f32[:],
                    start=False,
                    stop=(j == GPSIMD_BLOCKS - 1),
                )

        xt_of = {}
        for g in range(AHEAD):
            xt_of[g] = [transpose_half(g, 0), transpose_half(g, 1)]

        mean_var = const.tile([P, PACK, 2], F32)
        for e in range(2):
            nc.vector.bn_aggr(out=mean_var[:, e, :], in_=low_stats[:, early_calls : low_calls + 1, e, :])
        for e in range(2):
            nc.vector.tensor_scalar(
                out=mean_var[:, 2 + e, 0:1], in0=plain_sums[e][:, 0:1], scalar1=1.0 / ROWS, scalar2=None, op0=ALU.mult
            )
        off_centre = const.tile([P, 2], F32)
        nc.vector.tensor_tensor(out=off_centre[:], in0=mean_var[:, 2:4, 0], in1=neg_shift[:], op=ALU.add)
        off_centre_sq = const.tile([P, 2], F32)
        nc.vector.tensor_tensor(out=off_centre_sq[:], in0=off_centre[:], in1=off_centre[:], op=ALU.mult)
        high_square_sum = const.tile([P, 2], F32)
        nc.vector.tensor_reduce(out=high_square_sum[:], in_=square_sums[:], axis=AXIS.X, op=ALU.add)
        nc.vector.scalar_tensor_tensor(
            out=mean_var[:, 2:4, 1],
            in0=high_square_sum[:],
            scalar=1.0 / ROWS,
            in1=off_centre_sq[:],
            op0=ALU.mult,
            op1=ALU.subtract,
        )
        std = const.tile([P, PACK], F32)
        nc.scalar.activation(out=std[:], in_=mean_var[:, :, 1], func=FUNC.Sqrt, bias=eps[:], scale=1.0)
        inv_std = const.tile([P, PACK], F32)
        nc.vector.reciprocal(out=inv_std[:], in_=std[:])
        scale_k = const.tile([P, PACK], F32)
        nc.vector.tensor_tensor(out=scale_k[:], in0=gamma_beta[:, 0, :], in1=inv_std[:], op=ALU.mult)
        mean_scaled = const.tile([P, PACK], F32)
        nc.vector.tensor_tensor(out=mean_scaled[:], in0=mean_var[:, :, 0], in1=scale_k[:], op=ALU.mult)
        offset_k = const.tile([P, PACK], F32)
        nc.vector.tensor_tensor(out=offset_k[:], in0=gamma_beta[:, 1, :], in1=mean_scaled[:], op=ALU.subtract)

        w_grouped = const.tile([P, N_OUT, PACK], BF16, align_bytes=64)
        nc.vector.tensor_copy(out=w_grouped[:], in_=w_planes[:].rearrange("p t n -> p n t"))
        w_codes = const.tile([P, N_OUT], U32, align_bytes=64)
        w_scales = const.tile([P, N_OUT], U8, align_bytes=64)
        nc.vector.quantize_mx(
            out=w_codes[:].bitcast(FP8X4),
            scales=w_scales[:],
            in_=w_grouped[:].rearrange("p n t -> p (n t)"),
        )

        planes_of = {}
        grouped_of = {}
        acc_of = {}

        def normalise(g):
            planes = stage.tile([P, PACK, GROUP_ROWS], BF16, name="planes")
            for u in range(2):
                for e in range(2):
                    t = 2 * u + e
                    nc.scalar.activation(
                        out=planes[:, t, :],
                        in_=one_k(xt_of[g][u], e),
                        func=FUNC.Relu,
                        bias=offset_k[:, t : t + 1],
                        scale=scale_k[:, t : t + 1],
                    )
            planes_of[g] = planes

        def interleave(g):
            grouped = stage.tile([P, GROUP_ROWS, PACK], BF16, name="grouped", align_bytes=64)
            nc.vector.tensor_copy(
                out=grouped[:].rearrange("p (c i) t -> p c t i", i=4),
                in_=planes_of[g][:].rearrange("p t (c i) -> p c t i", i=4),
            )
            grouped_of[g] = grouped

        def quantise_and_multiply(g):
            codes = stage.tile([P, GROUP_ROWS], U32, name="codes", align_bytes=64)
            scales = stage.tile([P, GROUP_ROWS], U8, name="scales", align_bytes=64)
            nc.vector.quantize_mx(
                out=codes[:].bitcast(FP8X4),
                scales=scales[:],
                in_=grouped_of[g][:].rearrange("p r t -> p (r t)"),
            )
            acc = psum_acc.tile([P, GROUP, N_OUT], F32, name="acc")
            for j in range(GROUP):
                block = slice(j * P, (j + 1) * P)
                nc.tensor.matmul_mx(
                    out=acc[:, j, :],
                    lhsT=codes[:, block].bitcast(FP8X4),
                    lhsT_scale=scales[:, block],
                    rhs=w_codes[:].bitcast(FP8X4),
                    rhs_scale=w_scales[:],
                    start=True,
                    stop=True,
                )
            acc_of[g] = acc

        def add_bias_and_store(g):
            result = results.tile([P, GROUP, N_OUT], F32, name="result")
            nc.vector.tensor_tensor(
                out=result[:],
                in0=acc_of[g][:],
                in1=b_rows[:].unsqueeze(1).to_broadcast([P, GROUP, N_OUT]),
                op=ALU.add,
            )
            nc.sync.dma_start(out=out_dram[:, g * GROUP : (g + 1) * GROUP, :], in_=result[:])

        for s in range(GROUPS + 2):
            if s + AHEAD < GROUPS:
                xt_of[s + AHEAD] = [transpose_half(s + AHEAD, 0), transpose_half(s + AHEAD, 1)]
            if s < GROUPS:
                normalise(s)
                interleave(s)
            if 1 <= s <= GROUPS:
                quantise_and_multiply(s - 1)
            if s >= 2:
                add_bias_and_store(s - 2)
